import numpy as np
import ml_dtypes


def mxq(x, axis, fmt="e4m3"):
    dtype, down = {"e4m3": (ml_dtypes.float8_e4m3fn, 7), "e5m2": (ml_dtypes.float8_e5m2, 14)}[fmt]
    v = np.moveaxis(np.asarray(x, np.float32).astype(ml_dtypes.bfloat16).astype(np.float64), axis, -1)
    blocks = v.reshape(v.shape[:-1] + (-1, 32))
    amax = np.abs(blocks).max(-1, keepdims=True)
    byte = np.maximum(np.where(amax > 0, np.frexp(amax)[1] - 1 + 127, 0) - down, 1)
    scale = np.exp2(byte - 127.0)
    codes = (blocks / scale).astype(np.float32).astype(dtype).astype(np.float64)
    return np.moveaxis((codes * scale).reshape(v.shape), -1, axis)


WIDE = False


def mx_kscale(k):
    if not WIDE:
        return np.ones(k)
    levels = np.array([10, -10, 5, -5, 0])
    a = np.random.permutation(np.resize(levels, k // 512 * 4)).reshape(k // 512, 4)
    idx = np.arange(k)
    return np.exp2(a[idx // 512, idx % 128 // 32])


BF16 = ml_dtypes.bfloat16


def bf(x):
    return np.asarray(x, np.float32).astype(BF16)


def f64(x):
    return np.asarray(x).astype(np.float64)


E2M1 = np.array([0.0, 0.5, 1.0, 1.5, 2.0, 3.0, 4.0, 6.0, -0.0, -0.5, -1.0, -1.5, -2.0, -3.0, -4.0, -6.0])


def pack_weight(w, fmt):
    k, n = w.shape
    w = f64(bf(w)).reshape(k // 32, 32, n)
    amax = np.abs(w).max(1)
    if fmt == "e4m3":
        byte = np.frexp(amax)[1] - 1 + 127 - 7
    else:
        mant, ex = np.frexp(amax / 6.0)
        byte = np.where(mant > 0.5, ex, ex - 1) + 127
    byte = np.clip(np.where(amax > 0, byte, 1), 1, 254)
    scaled = (w * np.exp2(127.0 - byte)[:, None, :]).reshape(k, n).astype(np.float32)
    by_word = np.ascontiguousarray(scaled.reshape(k // 512, 128, 4, n).transpose(0, 1, 3, 2))
    if fmt == "e4m3":
        words = by_word.astype(ml_dtypes.float8_e4m3fn).view(np.uint8)
    else:
        c = by_word.astype(ml_dtypes.float4_e2m1fn).view(np.uint8) & 0xF
        words = c[..., 0::2] | (c[..., 1::2] << 4)
    return np.ascontiguousarray(words), np.ascontiguousarray(byte.astype(np.uint8).reshape(k // 512, 16, n))


def unpack_weight(words, scales, fmt):
    g, p, n, _ = words.shape
    if fmt == "e4m3":
        vals = np.ascontiguousarray(words).view(ml_dtypes.float8_e4m3fn).astype(np.float64)
    else:
        nib = np.empty((g, p, n, 4), np.uint8)
        nib[..., 0::2] = words & 0xF
        nib[..., 1::2] = words >> 4
        vals = E2M1[nib]
    vals = vals * np.repeat(np.exp2(scales.astype(np.float64) - 127.0), 8, axis=1)[..., None]
    return vals.transpose(0, 1, 3, 2).reshape(g * 512, n)


B, T, D, H, DH, F = 4, 32, 8192, 16, 64, 4096
A = H * DH
EPS = 1e-6
FMT = "e4m3"


def layer_norm(v, gain, bias):
    mu = v.mean(-1, keepdims=True)
    var = np.square(v - mu).mean(-1, keepdims=True)
    return (v - mu) * (1.0 / np.sqrt(var + EPS)) * gain + bias


def setup_inputs():
    s = mx_kscale(D)
    r = np.random.standard_normal
    x = bf(r((B, T, D)))
    ln1_gain = bf((1.0 + 0.1 * r(D)) * s)
    ln1_bias = bf(0.1 * r(D) * s)
    wq_words, wq_scales = pack_weight(r((D, A)) / np.sqrt(D) / s[:, None], FMT)
    bq = bf(0.1 * r(A))
    wk_words, wk_scales = pack_weight(r((D, A)) / np.sqrt(D) / s[:, None], FMT)
    bk = bf(0.1 * r(A))
    wv_words, wv_scales = pack_weight(r((D, A)) / np.sqrt(D) / s[:, None], FMT)
    bv = bf(0.1 * r(A))
    return {"x": x,
            "ln1_gain": ln1_gain,
            "ln1_bias": ln1_bias,
            "wq_words": wq_words,
            "wq_scales": wq_scales,
            "bq": bq,
            "wk_words": wk_words,
            "wk_scales": wk_scales,
            "bk": bk,
            "wv_words": wv_words,
            "wv_scales": wv_scales,
            "bv": bv}


def reference(x, ln1_gain, ln1_bias, wq_words, wq_scales, bq, wk_words, wk_scales, bk, wv_words, wv_scales, bv):
    h = layer_norm(f64(x), f64(ln1_gain), f64(ln1_bias))
    hq = mxq(h, 2, "e4m3")
    q = ((hq @ unpack_weight(wq_words, wq_scales, FMT)) + f64(bq)).reshape(B, T, H, DH)
    k = ((hq @ unpack_weight(wk_words, wk_scales, FMT)) + f64(bk)).reshape(B, T, H, DH)
    v = ((hq @ unpack_weight(wv_words, wv_scales, FMT)) + f64(bv)).reshape(B, T, H, DH)
    return q, k, v

@@ -1,0 +1,251 @@
+from contextlib import ExitStack
+
+import concourse.masks as masks
+import concourse.mybir as mybir
+
+F32 = mybir.dt.float32
+BF16 = mybir.dt.bfloat16
+I32 = mybir.dt.int32
+U32 = mybir.dt.uint32
+U8 = mybir.dt.uint8
+FP8X4 = mybir.dt.float8_e4m3fn_x4
+ALU = mybir.AluOpType
+ACT = mybir.ActivationFunctionType
+
+P = 128
+PACK = 4
+K_PASS = P * PACK
+D = 8192
+GROUPS = D // K_PASS
+A = 1024
+N_TILE = 512
+HALVES = A // N_TILE
+WEIGHTS = 3
+CHUNKS = WEIGHTS * GROUPS
+EPS = 1e-6
+
+X_TILES = 4
+X_COLS = D // X_TILES
+STAT_COLS = 512
+STATS_PER_TILE = X_COLS // STAT_COLS
+
+GAIN_ROW = 0
+BIAS_ROW = GROUPS
+OUT_BIAS_ROW = 2 * GROUPS
+
+RING = 2 * GROUPS
+
+REGROUP_LAG = 1
+QUANTISE_LAG = 2
+PROJECT_LAG = 3
+
+FLOPS = 2 * P * D * WEIGHTS * A
+
+
+def tile_swidtblock_pa_k_kernel(
+    tc, x, ln1_gain, ln1_bias, wq_words, wq_scales, bq, wk_words, wk_scales, bk,
+    wv_words, wv_scales, bv, out_0, out_1, out_2,
+):
+    nc = tc.nc
+    x_rows = x.rearrange("b t d -> (b t) d")
+    weight_words = [wq_words, wk_words, wv_words]
+    weight_scales = [wq_scales, wk_scales, wv_scales]
+    out_bias_vectors = [bq, bk, bv]
+    out_rows = [o.rearrange("b t h e -> (b t) (h e)") for o in [out_0, out_1, out_2]]
+
+    with ExitStack() as ctx:
+        ctx.enter_context(tc.manual_schedule())
+        keep = ctx.enter_context(tc.tile_pool(name="keep", bufs=1))
+        stage = ctx.enter_context(tc.tile_pool(name="stage", bufs=3))
+        results = ctx.enter_context(tc.tile_pool(name="results", bufs=4))
+        ring = ctx.enter_context(tc.tile_pool(name="ring", bufs=RING))
+        flip_banks = ctx.enter_context(tc.psum_pool(name="flip_banks", bufs=4))
+        sum_banks = ctx.enter_context(tc.psum_pool(name="sum_banks", bufs=2 * HALVES))
+
+        x_tiles = [keep.tile([P, X_COLS], BF16, name="x%d" % i) for i in range(X_TILES)]
+        for i in range(X_TILES):
+            nc.sync.dma_start(out=x_tiles[i][:], in_=x_rows[:, i * X_COLS : (i + 1) * X_COLS])
+
+        vec_rows = keep.tile([P, K_PASS], BF16)
+        nc.vector.memset(vec_rows[:].bitcast(I32), 0)
+        nc.scalar.dma_start(
+            out=vec_rows[GAIN_ROW : GAIN_ROW + GROUPS, :],
+            in_=ln1_gain.rearrange("(g c) -> g c", c=K_PASS),
+        )
+        nc.scalar.dma_start(
+            out=vec_rows[BIAS_ROW : BIAS_ROW + GROUPS, :],
+            in_=ln1_bias.rearrange("(g c) -> g c", c=K_PASS),
+        )
+        for w in range(WEIGHTS):
+            row = OUT_BIAS_ROW + HALVES * w
+            nc.scalar.dma_start(
+                out=vec_rows[row : row + HALVES, :],
+                in_=out_bias_vectors[w].rearrange("(r c) -> r c", c=N_TILE),
+            )
+
+        planes = keep.tile([P, GROUPS, A], U8, align_bytes=64)
+        nc.vector.memset(planes[:].rearrange("p g n -> p (g n)").bitcast(I32), 0)
+
+        identity = keep.tile([P, P], F32)
+        masks.make_identity(nc, identity[:])
+        identity_bf = keep.tile([P, P], BF16)
+        masks.make_identity(nc, identity_bf[:])
+
+        for w in range(WEIGHTS):
+            rows_first = weight_scales[w].bitcast(F32).rearrange("g q n -> q g n")
+            for quadrant in range(4):
+                first = 32 * quadrant + PACK * w
+                nc.gpsimd.dma_start(
+                    out=planes[first : first + 4, :, :].bitcast(F32),
+                    in_=rows_first[4 * quadrant : 4 * quadrant + 4, :, :],
+                )
+
+        chunk_words = {}
+
+        def load_chunk(c):
+            words = ring.tile([P, PACK * A], U8, align_bytes=64)
+            nc.sync.dma_start(
+                out=words[:].bitcast(I32),
+                in_=weight_words[c // GROUPS][c % GROUPS].rearrange("p n t -> p (n t)").bitcast(I32),
+            )
+            chunk_words[c] = words
+
+        for c in range(RING):
+            load_chunk(c)
+
+        vec_sorted = keep.tile([P, PACK, P], F32)
+        nc.scalar.copy(out=vec_sorted[:], in_=vec_rows[:].rearrange("r (p t) -> r t p", t=PACK))
+        vec_flipped = flip_banks.tile([P, PACK, P], F32, tag="flip")
+        for t in range(PACK):
+            nc.tensor.transpose(vec_flipped[:, t, :], vec_sorted[:, t, :], identity[:])
+        gain_bias = keep.tile([P, PACK, 2 * GROUPS], F32)
+        nc.scalar.copy(out=gain_bias[:], in_=vec_flipped[:, :, 0 : 2 * GROUPS])
+
+        out_bias = keep.tile([P, WEIGHTS * A], F32)
+        for j in range(WEIGHTS * HALVES):
+            r = OUT_BIAS_ROW + j
+            spread = flip_banks.tile([P, N_TILE], F32, tag="flip")
+            nc.tensor.matmul(
+                out=spread[:],
+                lhsT=identity_bf[:, r : r + 1].to_broadcast([P, P]),
+                rhs=vec_rows[:],
+                start=True,
+                stop=True,
+            )
+            nc.scalar.copy(out=out_bias[:, j * N_TILE : (j + 1) * N_TILE], in_=spread[:])
+
+        stats = keep.tile([P, X_TILES * STATS_PER_TILE, 6], F32)
+        for i in range(X_TILES):
+            for j in range(STATS_PER_TILE):
+                nc.vector.bn_stats(
+                    out=stats[:, i * STATS_PER_TILE + j, :],
+                    in_=x_tiles[i][:, j * STAT_COLS : (j + 1) * STAT_COLS],
+                )
+        mean_var = keep.tile([P, 2], F32)
+        nc.vector.bn_aggr(out=mean_var[:], in_=stats[:].rearrange("p c s -> p (c s)"))
+        var_eps = keep.tile([P, 1], F32)
+        nc.vector.tensor_scalar_add(out=var_eps[:], in0=mean_var[:, 1:2], scalar1=EPS)
+        std = keep.tile([P, 1], F32)
+        nc.scalar.sqrt(std[:], var_eps[:])
+        rstd = keep.tile([P, 1], F32)
+        nc.vector.reciprocal(out=rstd[:], in_=std[:])
+        shift = keep.tile([P, 1], F32)
+        nc.vector.scalar_tensor_tensor(
+            out=shift[:], in0=mean_var[:, 0:1], scalar=-1.0, in1=rstd[:], op0=ALU.mult, op1=ALU.mult
+        )
+
+        h_words = keep.tile([P, GROUPS, P], U32, align_bytes=64)
+        h_scales = keep.tile([P, GROUPS, P], U8, align_bytes=64)
+        scaled_tiles = {}
+        grouped_tiles = {}
+
+        def normalise_and_flip(g):
+            x_tile = x_tiles[g * K_PASS // X_COLS]
+            first = g * K_PASS % X_COLS
+            normal = stage.tile([P, PACK, P], F32)
+            nc.scalar.activation(
+                out=normal[:],
+                in_=x_tile[:, first : first + K_PASS].rearrange("m (p t) -> m t p", t=PACK),
+                func=ACT.Identity,
+                bias=shift[:],
+                scale=rstd[:],
+            )
+            flipped = flip_banks.tile([P, PACK, P], F32, tag="flip")
+            for t in range(PACK):
+                nc.tensor.transpose(flipped[:, t, :], normal[:, t, :], identity[:])
+            scaled = stage.tile([P, PACK, P], BF16)
+            for t in range(PACK):
+                nc.vector.tensor_scalar(
+                    out=scaled[:, t, :],
+                    in0=flipped[:, t, :],
+                    scalar1=gain_bias[:, t, GAIN_ROW + g : GAIN_ROW + g + 1],
+                    scalar2=gain_bias[:, t, BIAS_ROW + g : BIAS_ROW + g + 1],
+                    op0=ALU.mult,
+                    op1=ALU.add,
+                )
+            scaled_tiles[g] = scaled
+
+        def regroup(g):
+            grouped = stage.tile([P, P, PACK], BF16, align_bytes=64)
+            nc.vector.tensor_copy(out=grouped[:], in_=scaled_tiles[g][:].rearrange("p t m -> p m t"))
+            grouped_tiles[g] = grouped
+
+        def quantise(g):
+            nc.vector.quantize_mx(
+                out=h_words[:, g, :].bitcast(FP8X4),
+                scales=h_scales[:, g, :],
+                in_=grouped_tiles[g][:].rearrange("p m t -> p (m t)"),
+            )
+
+        sums = {}
+
+        def open_sums(w):
+            for half in range(HALVES):
+                sums[(w, half)] = sum_banks.tile([P, N_TILE], F32, name="sum", tag="sum")
+
+        def project(w, g):
+            c = w * GROUPS + g
+            words = chunk_words[c]
+            for half in range(HALVES):
+                nc.tensor.matmul_mx(
+                    out=sums[(w, half)][:],
+                    lhsT=h_words[:, g, :].bitcast(FP8X4),
+                    lhsT_scale=h_scales[:, g, :],
+                    rhs=words[:, half * PACK * N_TILE : (half + 1) * PACK * N_TILE].bitcast(FP8X4),
+                    rhs_scale=planes[PACK * w : P, g, half * N_TILE : (half + 1) * N_TILE],
+                    start=(g == 0),
+                    stop=(g == GROUPS - 1),
+                )
+            if c + RING < CHUNKS:
+                load_chunk(c + RING)
+
+        def add_bias_and_store(w):
+            for half in range(HALVES):
+                result = results.tile([P, N_TILE], F32)
+                nc.vector.tensor_tensor(
+                    out=result[:],
+                    in0=sums[(w, half)][:],
+                    in1=out_bias[:, w * A + half * N_TILE : w * A + (half + 1) * N_TILE],
+                    op=ALU.add,
+                )
+                nc.scalar.dma_start(
+                    out=out_rows[w][:, half * N_TILE : (half + 1) * N_TILE], in_=result[:]
+                )
+
+        open_sums(0)
+        for s in range(GROUPS + PROJECT_LAG):
+            if s < GROUPS:
+                normalise_and_flip(s)
+            if 0 <= s - REGROUP_LAG < GROUPS:
+                regroup(s - REGROUP_LAG)
+            if 0 <= s - QUANTISE_LAG < GROUPS:
+                quantise(s - QUANTISE_LAG)
+            if 0 <= s - PROJECT_LAG:
+                project(0, s - PROJECT_LAG)
+        add_bias_and_store(0)
+
+        for w in range(1, WEIGHTS):
+            open_sums(w)
+            for g in range(GROUPS):
+                project(w, g)
+            add_bias_and_store(w)

@@ -35,9 +35,8 @@ OUT_BIAS_ROW = 2 * GROUPS
 
 RING = 2 * GROUPS
 
-REGROUP_LAG = 1
-QUANTISE_LAG = 2
-PROJECT_LAG = 3
+BLOCK = 4
+BLOCKS = GROUPS // BLOCK
 
 FLOPS = 2 * P * D * WEIGHTS * A
 
@@ -56,10 +55,11 @@ def tile_swidtblock_pa_k_kernel(
     with ExitStack() as ctx:
         ctx.enter_context(tc.manual_schedule())
         keep = ctx.enter_context(tc.tile_pool(name="keep", bufs=1))
-        stage = ctx.enter_context(tc.tile_pool(name="stage", bufs=3))
-        results = ctx.enter_context(tc.tile_pool(name="results", bufs=4))
+        normals = ctx.enter_context(tc.tile_pool(name="normals", bufs=BLOCK + 2))
+        stage = ctx.enter_context(tc.tile_pool(name="stage", bufs=2))
+        results = ctx.enter_context(tc.tile_pool(name="results", bufs=HALVES))
         ring = ctx.enter_context(tc.tile_pool(name="ring", bufs=RING))
-        flip_banks = ctx.enter_context(tc.psum_pool(name="flip_banks", bufs=4))
+        flip_banks = ctx.enter_context(tc.psum_pool(name="flip_banks", bufs=BLOCK))
         sum_banks = ctx.enter_context(tc.psum_pool(name="sum_banks", bufs=2 * HALVES))
 
         x_tiles = [keep.tile([P, X_COLS], BF16, name="x%d" % i) for i in range(X_TILES)]
@@ -159,42 +159,47 @@ def tile_swidtblock_pa_k_kernel(
         scaled_tiles = {}
         grouped_tiles = {}
 
-        def normalise_and_flip(g):
-            x_tile = x_tiles[g * K_PASS // X_COLS]
-            first = g * K_PASS % X_COLS
-            normal = stage.tile([P, PACK, P], F32)
-            nc.scalar.activation(
-                out=normal[:],
-                in_=x_tile[:, first : first + K_PASS].rearrange("m (p t) -> m t p", t=PACK),
-                func=ACT.Identity,
-                bias=shift[:],
-                scale=rstd[:],
-            )
-            flipped = flip_banks.tile([P, PACK, P], F32, tag="flip")
-            for t in range(PACK):
-                nc.tensor.transpose(flipped[:, t, :], normal[:, t, :], identity[:])
-            scaled = stage.tile([P, PACK, P], BF16)
-            for t in range(PACK):
-                nc.vector.tensor_scalar(
-                    out=scaled[:, t, :],
-                    in0=flipped[:, t, :],
-                    scalar1=gain_bias[:, t, GAIN_ROW + g : GAIN_ROW + g + 1],
-                    scalar2=gain_bias[:, t, BIAS_ROW + g : BIAS_ROW + g + 1],
-                    op0=ALU.mult,
-                    op1=ALU.add,
+        def normalise_flip_scale(b):
+            scaled = stage.tile([P, BLOCK, PACK, P], BF16)
+            for i in range(BLOCK):
+                g = b * BLOCK + i
+                normal = normals.tile([P, PACK, P], F32)
+                nc.scalar.activation(
+                    out=normal[:],
+                    in_=x_tiles[b][:, i * K_PASS : (i + 1) * K_PASS].rearrange(
+                        "m (p t) -> m t p", t=PACK
+                    ),
+                    func=ACT.Identity,
+                    bias=shift[:],
+                    scale=rstd[:],
                 )
-            scaled_tiles[g] = scaled
+                flipped = flip_banks.tile([P, PACK, P], F32, tag="flip")
+                for t in range(PACK):
+                    nc.tensor.transpose(flipped[:, t, :], normal[:, t, :], identity[:])
+                for t in range(PACK):
+                    nc.vector.tensor_scalar(
+                        out=scaled[:, i, t, :],
+                        in0=flipped[:, t, :],
+                        scalar1=gain_bias[:, t, GAIN_ROW + g : GAIN_ROW + g + 1],
+                        scalar2=gain_bias[:, t, BIAS_ROW + g : BIAS_ROW + g + 1],
+                        op0=ALU.mult,
+                        op1=ALU.add,
+                    )
+            scaled_tiles[b] = scaled
 
-        def regroup(g):
-            grouped = stage.tile([P, P, PACK], BF16, align_bytes=64)
-            nc.vector.tensor_copy(out=grouped[:], in_=scaled_tiles[g][:].rearrange("p t m -> p m t"))
-            grouped_tiles[g] = grouped
+        def regroup(b):
+            grouped = stage.tile([P, BLOCK, P, PACK], BF16, align_bytes=64)
+            nc.vector.tensor_copy(
+                out=grouped[:], in_=scaled_tiles[b][:].rearrange("p i t m -> p i m t")
+            )
+            grouped_tiles[b] = grouped
 
-        def quantise(g):
+        def quantise(b):
+            groups = slice(b * BLOCK, (b + 1) * BLOCK)
             nc.vector.quantize_mx(
-                out=h_words[:, g, :].bitcast(FP8X4),
-                scales=h_scales[:, g, :],
-                in_=grouped_tiles[g][:].rearrange("p m t -> p (m t)"),
+                out=h_words[:, groups, :].rearrange("p i m -> p (i m)").bitcast(FP8X4),
+                scales=h_scales[:, groups, :].rearrange("p i m -> p (i m)"),
+                in_=grouped_tiles[b][:].rearrange("p i m t -> p (i m t)"),
             )
 
         sums = {}
@@ -233,15 +238,16 @@ def tile_swidtblock_pa_k_kernel(
                 )
 
         open_sums(0)
-        for s in range(GROUPS + PROJECT_LAG):
-            if s < GROUPS:
-                normalise_and_flip(s)
-            if 0 <= s - REGROUP_LAG < GROUPS:
-                regroup(s - REGROUP_LAG)
-            if 0 <= s - QUANTISE_LAG < GROUPS:
-                quantise(s - QUANTISE_LAG)
-            if 0 <= s - PROJECT_LAG:
-                project(0, s - PROJECT_LAG)
+        for b in range(BLOCKS + 2):
+            if b < BLOCKS:
+                normalise_flip_scale(b)
+            if 1 <= b <= BLOCKS:
+                quantise(b - 1)
+            if b < BLOCKS:
+                regroup(b)
+            if b >= 2:
+                for i in range(BLOCK):
+                    project(0, (b - 2) * BLOCK + i)
         add_bias_and_store(0)
 
         for w in range(1, WEIGHTS):

@@ -92,11 +92,11 @@ def tile_swidtblock_pa_k_kernel(
         masks.make_identity(nc, identity_bf[:])
 
         for w in range(WEIGHTS):
-            rows_first = weight_scales[w].bitcast(F32).rearrange("g q n -> q g n")
+            rows_first = weight_scales[w].bitcast(I32).rearrange("g q n -> q g n")
             for quadrant in range(4):
                 first = 32 * quadrant + PACK * w
-                nc.gpsimd.dma_start(
-                    out=planes[first : first + 4, :, :].bitcast(F32),
+                nc.sync.dma_start(
+                    out=planes[first : first + 4, :, :].bitcast(I32),
                     in_=rows_first[4 * quadrant : 4 * quadrant + 4, :, :],
                 )
 

@@ -83,8 +83,8 @@ def tile_swidtblock_pa_k_kernel(
                 in_=out_bias_vectors[w].rearrange("(r c) -> r c", c=N_TILE),
             )
 
-        planes = keep.tile([P, GROUPS, A], U8, align_bytes=64)
-        nc.vector.memset(planes[:].rearrange("p g n -> p (g n)").bitcast(I32), 0)
+        planes = keep.tile([P, WEIGHTS, BLOCKS, A], U8, align_bytes=64)
+        nc.vector.memset(planes[:].rearrange("p w j n -> p (w j n)").bitcast(I32), 0)
 
         identity = keep.tile([P, P], F32)
         masks.make_identity(nc, identity[:])
@@ -92,13 +92,14 @@ def tile_swidtblock_pa_k_kernel(
         masks.make_identity(nc, identity_bf[:])
 
         for w in range(WEIGHTS):
-            rows_first = weight_scales[w].bitcast(I32).rearrange("g q n -> q g n")
-            for quadrant in range(4):
-                first = 32 * quadrant + PACK * w
-                nc.sync.dma_start(
-                    out=planes[first : first + 4, :, :].bitcast(I32),
-                    in_=rows_first[4 * quadrant : 4 * quadrant + 4, :, :],
-                )
+            for j in range(BLOCKS):
+                for quadrant in range(4):
+                    nc.sync.dma_start(
+                        out=planes[32 * quadrant : 32 * quadrant + 16, w, j, :].bitcast(I32),
+                        in_=weight_scales[w][
+                            BLOCK * j : BLOCK * (j + 1), 4 * quadrant : 4 * quadrant + 4, :
+                        ].bitcast(I32),
+                    )
 
         chunk_words = {}
 
@@ -217,7 +218,9 @@ def tile_swidtblock_pa_k_kernel(
                     lhsT=h_words[:, g, :].bitcast(FP8X4),
                     lhsT_scale=h_scales[:, g, :],
                     rhs=words[:, half * PACK * N_TILE : (half + 1) * PACK * N_TILE].bitcast(FP8X4),
-                    rhs_scale=planes[PACK * w : P, g, half * N_TILE : (half + 1) * N_TILE],
+                    rhs_scale=planes[
+                        4 * (g % BLOCK) : P, w, g // BLOCK, half * N_TILE : (half + 1) * N_TILE
+                    ],
                     start=(g == 0),
                     stop=(g == GROUPS - 1),
                 )

@@ -94,11 +94,11 @@ def tile_swidtblock_pa_k_kernel(
         for w in range(WEIGHTS):
             for j in range(BLOCKS):
                 for quadrant in range(4):
-                    nc.sync.dma_start(
-                        out=planes[32 * quadrant : 32 * quadrant + 16, w, j, :].bitcast(I32),
+                    nc.gpsimd.dma_start(
+                        out=planes[32 * quadrant : 32 * quadrant + 16, w, j, :].bitcast(F32),
                         in_=weight_scales[w][
                             BLOCK * j : BLOCK * (j + 1), 4 * quadrant : 4 * quadrant + 4, :
-                        ].bitcast(I32),
+                        ].bitcast(F32),
                     )
 
         chunk_words = {}

@@ -57,7 +57,7 @@ def tile_swidtblock_pa_k_kernel(
         keep = ctx.enter_context(tc.tile_pool(name="keep", bufs=1))
         normals = ctx.enter_context(tc.tile_pool(name="normals", bufs=BLOCK + 2))
         stage = ctx.enter_context(tc.tile_pool(name="stage", bufs=2))
-        results = ctx.enter_context(tc.tile_pool(name="results", bufs=HALVES))
+        results = ctx.enter_context(tc.tile_pool(name="results", bufs=WEIGHTS))
         ring = ctx.enter_context(tc.tile_pool(name="ring", bufs=RING))
         flip_banks = ctx.enter_context(tc.psum_pool(name="flip_banks", bufs=BLOCK))
         sum_banks = ctx.enter_context(tc.psum_pool(name="sum_banks", bufs=2 * HALVES))
@@ -105,10 +105,12 @@ def tile_swidtblock_pa_k_kernel(
 
         def load_chunk(c):
             words = ring.tile([P, PACK * A], U8, align_bytes=64)
-            nc.sync.dma_start(
-                out=words[:].bitcast(I32),
-                in_=weight_words[c // GROUPS][c % GROUPS].rearrange("p n t -> p (n t)").bitcast(I32),
-            )
+            source = weight_words[c // GROUPS][c % GROUPS].rearrange("p n t -> p (n t)")
+            pieces = HALVES if c == CHUNKS - 1 else 1
+            width = PACK * A // pieces
+            for i in range(pieces):
+                cols = slice(i * width, (i + 1) * width)
+                nc.sync.dma_start(out=words[:, cols].bitcast(I32), in_=source[:, cols].bitcast(I32))
             chunk_words[c] = words
 
         for c in range(RING):
@@ -228,17 +230,19 @@ def tile_swidtblock_pa_k_kernel(
                 load_chunk(c + RING)
 
         def add_bias_and_store(w):
+            result = results.tile([P, A], F32)
             for half in range(HALVES):
-                result = results.tile([P, N_TILE], F32)
+                cols = slice(half * N_TILE, (half + 1) * N_TILE)
                 nc.vector.tensor_tensor(
-                    out=result[:],
+                    out=result[:, cols],
                     in0=sums[(w, half)][:],
                     in1=out_bias[:, w * A + half * N_TILE : w * A + (half + 1) * N_TILE],
                     op=ALU.add,
                 )
-                nc.scalar.dma_start(
-                    out=out_rows[w][:, half * N_TILE : (half + 1) * N_TILE], in_=result[:]
-                )
+                if w == WEIGHTS - 1:
+                    nc.scalar.dma_start(out=out_rows[w][:, cols], in_=result[:, cols])
+            if w < WEIGHTS - 1:
+                nc.sync.dma_start(out=out_rows[w], in_=result[:])
 
         open_sums(0)
         for b in range(BLOCKS + 2):

@@ -20,12 +20,14 @@ GROUPS = D // K_PASS
 A = 1024
 N_TILE = 512
 HALVES = A // N_TILE
+COLUMNS = [[N_TILE] * HALVES, [N_TILE] * HALVES, [N_TILE, N_TILE // 2, N_TILE // 2]]
 WEIGHTS = 3
 CHUNKS = WEIGHTS * GROUPS
 EPS = 1e-6
 
-X_TILES = 4
+X_TILES = 2
 X_COLS = D // X_TILES
+X_GROUPS = GROUPS // X_TILES
 STAT_COLS = 512
 STATS_PER_TILE = X_COLS // STAT_COLS
 
@@ -106,11 +108,11 @@ def tile_swidtblock_pa_k_kernel(
         def load_chunk(c):
             words = ring.tile([P, PACK * A], U8, align_bytes=64)
             source = weight_words[c // GROUPS][c % GROUPS].rearrange("p n t -> p (n t)")
-            pieces = HALVES if c == CHUNKS - 1 else 1
-            width = PACK * A // pieces
-            for i in range(pieces):
-                cols = slice(i * width, (i + 1) * width)
+            start = 0
+            for width in COLUMNS[-1] if c == CHUNKS - 1 else [A]:
+                cols = slice(PACK * start, PACK * (start + width))
                 nc.sync.dma_start(out=words[:, cols].bitcast(I32), in_=source[:, cols].bitcast(I32))
+                start += width
             chunk_words[c] = words
 
         for c in range(RING):
@@ -169,9 +171,9 @@ def tile_swidtblock_pa_k_kernel(
                 normal = normals.tile([P, PACK, P], F32)
                 nc.scalar.activation(
                     out=normal[:],
-                    in_=x_tiles[b][:, i * K_PASS : (i + 1) * K_PASS].rearrange(
-                        "m (p t) -> m t p", t=PACK
-                    ),
+                    in_=x_tiles[g // X_GROUPS][
+                        :, g % X_GROUPS * K_PASS : (g % X_GROUPS + 1) * K_PASS
+                    ].rearrange("m (p t) -> m t p", t=PACK),
                     func=ACT.Identity,
                     bias=shift[:],
                     scale=rstd[:],
@@ -208,21 +210,26 @@ def tile_swidtblock_pa_k_kernel(
         sums = {}
 
         def open_sums(w):
-            for half in range(HALVES):
-                sums[(w, half)] = sum_banks.tile([P, N_TILE], F32, name="sum", tag="sum")
+            sums[w] = []
+            start = 0
+            for i, width in enumerate(COLUMNS[w]):
+                if i < HALVES:
+                    bank = sum_banks.tile([P, N_TILE], F32, name="sum", tag="sum")
+                else:
+                    bank = flip_banks.tile([P, N_TILE], F32, name="flip", tag="flip")
+                sums[w].append((start, start + width, bank[:, 0:width]))
+                start += width
 
         def project(w, g):
             c = w * GROUPS + g
             words = chunk_words[c]
-            for half in range(HALVES):
+            for lo, hi, sum_of_piece in sums[w]:
                 nc.tensor.matmul_mx(
-                    out=sums[(w, half)][:],
+                    out=sum_of_piece,
                     lhsT=h_words[:, g, :].bitcast(FP8X4),
                     lhsT_scale=h_scales[:, g, :],
-                    rhs=words[:, half * PACK * N_TILE : (half + 1) * PACK * N_TILE].bitcast(FP8X4),
-                    rhs_scale=planes[
-                        4 * (g % BLOCK) : P, w, g // BLOCK, half * N_TILE : (half + 1) * N_TILE
-                    ],
+                    rhs=words[:, PACK * lo : PACK * hi].bitcast(FP8X4),
+                    rhs_scale=planes[4 * (g % BLOCK) : P, w, g // BLOCK, lo:hi],
                     start=(g == 0),
                     stop=(g == GROUPS - 1),
                 )
@@ -231,16 +238,15 @@ def tile_swidtblock_pa_k_kernel(
 
         def add_bias_and_store(w):
             result = results.tile([P, A], F32)
-            for half in range(HALVES):
-                cols = slice(half * N_TILE, (half + 1) * N_TILE)
+            for lo, hi, sum_of_piece in sums[w]:
                 nc.vector.tensor_tensor(
-                    out=result[:, cols],
-                    in0=sums[(w, half)][:],
-                    in1=out_bias[:, w * A + half * N_TILE : w * A + (half + 1) * N_TILE],
+                    out=result[:, lo:hi],
+                    in0=sum_of_piece,
+                    in1=out_bias[:, w * A + lo : w * A + hi],
                     op=ALU.add,
                 )
                 if w == WEIGHTS - 1:
-                    nc.scalar.dma_start(out=out_rows[w][:, cols], in_=result[:, cols])
+                    nc.scalar.dma_start(out=out_rows[w][:, lo:hi], in_=result[:, lo:hi])
             if w < WEIGHTS - 1:
                 nc.sync.dma_start(out=out_rows[w], in_=result[:])
 

@@ -85,23 +85,10 @@ def tile_swidtblock_pa_k_kernel(
                 in_=out_bias_vectors[w].rearrange("(r c) -> r c", c=N_TILE),
             )
 
-        planes = keep.tile([P, WEIGHTS, BLOCKS, A], U8, align_bytes=64)
-        nc.vector.memset(planes[:].rearrange("p w j n -> p (w j n)").bitcast(I32), 0)
-
         identity = keep.tile([P, P], F32)
         masks.make_identity(nc, identity[:])
         identity_bf = keep.tile([P, P], BF16)
         masks.make_identity(nc, identity_bf[:])
-
-        for w in range(WEIGHTS):
-            for j in range(BLOCKS):
-                for quadrant in range(4):
-                    nc.gpsimd.dma_start(
-                        out=planes[32 * quadrant : 32 * quadrant + 16, w, j, :].bitcast(F32),
-                        in_=weight_scales[w][
-                            BLOCK * j : BLOCK * (j + 1), 4 * quadrant : 4 * quadrant + 4, :
-                        ].bitcast(F32),
-                    )
 
         chunk_words = {}
 
@@ -140,12 +127,30 @@ def tile_swidtblock_pa_k_kernel(
             nc.scalar.copy(out=out_bias[:, j * N_TILE : (j + 1) * N_TILE], in_=spread[:])
 
         stats = keep.tile([P, X_TILES * STATS_PER_TILE, 6], F32)
-        for i in range(X_TILES):
+
+        def take_statistics(i):
             for j in range(STATS_PER_TILE):
                 nc.vector.bn_stats(
                     out=stats[:, i * STATS_PER_TILE + j, :],
                     in_=x_tiles[i][:, j * STAT_COLS : (j + 1) * STAT_COLS],
                 )
+
+        take_statistics(0)
+
+        planes = keep.tile([P, WEIGHTS, BLOCKS, A], U8, align_bytes=64)
+        nc.vector.memset(planes[:].rearrange("p w j n -> p (w j n)").bitcast(I32), 0)
+
+        for w in range(WEIGHTS):
+            for j in range(BLOCKS):
+                for quadrant in range(4):
+                    nc.gpsimd.dma_start(
+                        out=planes[32 * quadrant : 32 * quadrant + 16, w, j, :].bitcast(F32),
+                        in_=weight_scales[w][
+                            BLOCK * j : BLOCK * (j + 1), 4 * quadrant : 4 * quadrant + 4, :
+                        ].bitcast(F32),
+                    )
+
+        take_statistics(1)
         mean_var = keep.tile([P, 2], F32)
         nc.vector.bn_aggr(out=mean_var[:], in_=stats[:].rearrange("p c s -> p (c s)"))
         var_eps = keep.tile([P, 1], F32)

@@ -40,6 +40,8 @@ RING = 2 * GROUPS
 BLOCK = 4
 BLOCKS = GROUPS // BLOCK
 
+LATE = 2
+
 FLOPS = 2 * P * D * WEIGHTS * A
 
 
@@ -92,15 +94,26 @@ def tile_swidtblock_pa_k_kernel(
 
         chunk_words = {}
 
-        def load_chunk(c):
-            words = ring.tile([P, PACK * A], U8, align_bytes=64)
+        def load_columns(c, lo, hi):
             source = weight_words[c // GROUPS][c % GROUPS].rearrange("p n t -> p (n t)")
-            start = 0
-            for width in COLUMNS[-1] if c == CHUNKS - 1 else [A]:
-                cols = slice(PACK * start, PACK * (start + width))
-                nc.sync.dma_start(out=words[:, cols].bitcast(I32), in_=source[:, cols].bitcast(I32))
-                start += width
-            chunk_words[c] = words
+            cols = slice(PACK * lo, PACK * hi)
+            nc.sync.dma_start(
+                out=chunk_words[c][:, cols].bitcast(I32), in_=source[:, cols].bitcast(I32)
+            )
+
+        def load_chunk(c):
+            chunk_words[c] = ring.tile([P, PACK * A], U8, name="words", align_bytes=64)
+            if c < CHUNKS - LATE:
+                load_columns(c, 0, A)
+                return
+            load_columns(c, 0, N_TILE)
+            if c == CHUNKS - 1:
+                for late in range(CHUNKS - LATE, CHUNKS):
+                    pieces = COLUMNS[-1][1:] if late == CHUNKS - 1 else [A - N_TILE]
+                    start = N_TILE
+                    for width in pieces:
+                        load_columns(late, start, start + width)
+                        start += width
 
         for c in range(RING):
             load_chunk(c)
@@ -225,10 +238,10 @@ def tile_swidtblock_pa_k_kernel(
                 sums[w].append((start, start + width, bank[:, 0:width]))
                 start += width
 
-        def project(w, g):
+        def project(w, g, pieces=slice(None)):
             c = w * GROUPS + g
             words = chunk_words[c]
-            for lo, hi, sum_of_piece in sums[w]:
+            for lo, hi, sum_of_piece in sums[w][pieces]:
                 nc.tensor.matmul_mx(
                     out=sum_of_piece,
                     lhsT=h_words[:, g, :].bitcast(FP8X4),
@@ -270,6 +283,10 @@ def tile_swidtblock_pa_k_kernel(
 
         for w in range(1, WEIGHTS):
             open_sums(w)
-            for g in range(GROUPS):
+            late = LATE if w == WEIGHTS - 1 else 0
+            for g in range(GROUPS - late):
                 project(w, g)
+            for pieces in [slice(0, 1), slice(1, None)]:
+                for g in range(GROUPS - late, GROUPS):
+                    project(w, g, pieces)
             add_bias_and_store(w)

@@ -66,7 +66,7 @@ def tile_swidtblock_pa_k_kernel(
         flip_banks = ctx.enter_context(tc.psum_pool(name="flip_banks", bufs=BLOCK))
         sum_banks = ctx.enter_context(tc.psum_pool(name="sum_banks", bufs=2 * HALVES))
 
-        x_tiles = [keep.tile([P, X_COLS], BF16, name="x%d" % i) for i in range(X_TILES)]
+        x_tiles = [keep.tile([P, X_COLS], BF16, name="x%d" % i, align_bytes=512) for i in range(X_TILES)]
         for i in range(X_TILES):
             nc.sync.dma_start(out=x_tiles[i][:], in_=x_rows[:, i * X_COLS : (i + 1) * X_COLS])
 
@@ -102,7 +102,7 @@ def tile_swidtblock_pa_k_kernel(
             )
 
         def load_chunk(c):
-            chunk_words[c] = ring.tile([P, PACK * A], U8, name="words", align_bytes=64)
+            chunk_words[c] = ring.tile([P, PACK * A], U8, name="words", align_bytes=512)
             if c < CHUNKS - LATE:
                 load_columns(c, 0, A)
                 return
@@ -150,7 +150,7 @@ def tile_swidtblock_pa_k_kernel(
 
         take_statistics(0)
 
-        planes = keep.tile([P, WEIGHTS, BLOCKS, A], U8, align_bytes=64)
+        planes = keep.tile([P, WEIGHTS, BLOCKS, A], U8, align_bytes=512)
         nc.vector.memset(planes[:].rearrange("p w j n -> p (w j n)").bitcast(I32), 0)
 
         for w in range(WEIGHTS):
@@ -255,7 +255,7 @@ def tile_swidtblock_pa_k_kernel(
                 load_chunk(c + RING)
 
         def add_bias_and_store(w):
-            result = results.tile([P, A], F32)
+            result = results.tile([P, A], F32, align_bytes=512)
             for lo, hi, sum_of_piece in sums[w]:
                 nc.vector.tensor_tensor(
                     out=result[:, lo:hi],

@@ -66,7 +66,7 @@ def tile_swidtblock_pa_k_kernel(
         flip_banks = ctx.enter_context(tc.psum_pool(name="flip_banks", bufs=BLOCK))
         sum_banks = ctx.enter_context(tc.psum_pool(name="sum_banks", bufs=2 * HALVES))
 
-        x_tiles = [keep.tile([P, X_COLS], BF16, name="x%d" % i, align_bytes=512) for i in range(X_TILES)]
+        x_tiles = [keep.tile([P, X_COLS], BF16, name="x%d" % i, align_bytes=4096) for i in range(X_TILES)]
         for i in range(X_TILES):
             nc.sync.dma_start(out=x_tiles[i][:], in_=x_rows[:, i * X_COLS : (i + 1) * X_COLS])
 
@@ -102,7 +102,7 @@ def tile_swidtblock_pa_k_kernel(
             )
 
         def load_chunk(c):
-            chunk_words[c] = ring.tile([P, PACK * A], U8, name="words", align_bytes=512)
+            chunk_words[c] = ring.tile([P, PACK * A], U8, name="words", align_bytes=4096)
             if c < CHUNKS - LATE:
                 load_columns(c, 0, A)
                 return
@@ -150,7 +150,7 @@ def tile_swidtblock_pa_k_kernel(
 
         take_statistics(0)
 
-        planes = keep.tile([P, WEIGHTS, BLOCKS, A], U8, align_bytes=512)
+        planes = keep.tile([P, WEIGHTS, BLOCKS, A], U8, align_bytes=1024)
         nc.vector.memset(planes[:].rearrange("p w j n -> p (w j n)").bitcast(I32), 0)
 
         for w in range(WEIGHTS):
@@ -255,7 +255,7 @@ def tile_swidtblock_pa_k_kernel(
                 load_chunk(c + RING)
 
         def add_bias_and_store(w):
-            result = results.tile([P, A], F32, align_bytes=512)
+            result = results.tile([P, A], F32, align_bytes=1024)
             for lo, hi, sum_of_piece in sums[w]:
                 nc.vector.tensor_tensor(
                     out=result[:, lo:hi],

@@ -155,11 +155,15 @@ def tile_swidtblock_pa_k_kernel(
 
         for w in range(WEIGHTS):
             for j in range(BLOCKS):
-                for quadrant in range(4):
+                last = j == BLOCKS - 1
+                groups = BLOCK if last else 2 * BLOCK
+                for quadrant in (0, 1, 2, 3) if last else (0, 2, 1, 3):
                     nc.gpsimd.dma_start(
-                        out=planes[32 * quadrant : 32 * quadrant + 16, w, j, :].bitcast(F32),
+                        out=planes[
+                            32 * quadrant : 32 * quadrant + 4 * groups, w, j, :
+                        ].bitcast(F32),
                         in_=weight_scales[w][
-                            BLOCK * j : BLOCK * (j + 1), 4 * quadrant : 4 * quadrant + 4, :
+                            BLOCK * j : BLOCK * j + groups, 4 * quadrant : 4 * quadrant + 4, :
                         ].bitcast(F32),
                     )
 

from contextlib import ExitStack

import concourse.masks as masks
import concourse.mybir as mybir

F32 = mybir.dt.float32
BF16 = mybir.dt.bfloat16
I32 = mybir.dt.int32
U32 = mybir.dt.uint32
U8 = mybir.dt.uint8
FP8X4 = mybir.dt.float8_e4m3fn_x4
ALU = mybir.AluOpType
ACT = mybir.ActivationFunctionType

P = 128
PACK = 4
K_PASS = P * PACK
D = 8192
GROUPS = D // K_PASS
A = 1024
N_TILE = 512
HALVES = A // N_TILE
COLUMNS = [[N_TILE] * HALVES, [N_TILE] * HALVES, [N_TILE, N_TILE // 2, N_TILE // 2]]
WEIGHTS = 3
CHUNKS = WEIGHTS * GROUPS
EPS = 1e-6

X_TILES = 2
X_COLS = D // X_TILES
X_GROUPS = GROUPS // X_TILES
STAT_COLS = 512
STATS_PER_TILE = X_COLS // STAT_COLS

GAIN_ROW = 0
BIAS_ROW = GROUPS
OUT_BIAS_ROW = 2 * GROUPS

RING = 2 * GROUPS

BLOCK = 4
BLOCKS = GROUPS // BLOCK

LATE = 2

FLOPS = 2 * P * D * WEIGHTS * A


def tile_swidtblock_pa_k_kernel(
    tc, x, ln1_gain, ln1_bias, wq_words, wq_scales, bq, wk_words, wk_scales, bk,
    wv_words, wv_scales, bv, out_0, out_1, out_2,
):
    nc = tc.nc
    x_rows = x.rearrange("b t d -> (b t) d")
    weight_words = [wq_words, wk_words, wv_words]
    weight_scales = [wq_scales, wk_scales, wv_scales]
    out_bias_vectors = [bq, bk, bv]
    out_rows = [o.rearrange("b t h e -> (b t) (h e)") for o in [out_0, out_1, out_2]]

    with ExitStack() as ctx:
        ctx.enter_context(tc.manual_schedule())
        keep = ctx.enter_context(tc.tile_pool(name="keep", bufs=1))
        normals = ctx.enter_context(tc.tile_pool(name="normals", bufs=BLOCK + 2))
        stage = ctx.enter_context(tc.tile_pool(name="stage", bufs=2))
        results = ctx.enter_context(tc.tile_pool(name="results", bufs=WEIGHTS))
        ring = ctx.enter_context(tc.tile_pool(name="ring", bufs=RING))
        flip_banks = ctx.enter_context(tc.psum_pool(name="flip_banks", bufs=BLOCK))
        sum_banks = ctx.enter_context(tc.psum_pool(name="sum_banks", bufs=2 * HALVES))

        x_tiles = [keep.tile([P, X_COLS], BF16, name="x%d" % i, align_bytes=4096) for i in range(X_TILES)]
        for i in range(X_TILES):
            nc.sync.dma_start(out=x_tiles[i][:], in_=x_rows[:, i * X_COLS : (i + 1) * X_COLS])

        vec_rows = keep.tile([P, K_PASS], BF16)
        nc.vector.memset(vec_rows[:].bitcast(I32), 0)
        nc.scalar.dma_start(
            out=vec_rows[GAIN_ROW : GAIN_ROW + GROUPS, :],
            in_=ln1_gain.rearrange("(g c) -> g c", c=K_PASS),
        )
        nc.scalar.dma_start(
            out=vec_rows[BIAS_ROW : BIAS_ROW + GROUPS, :],
            in_=ln1_bias.rearrange("(g c) -> g c", c=K_PASS),
        )
        for w in range(WEIGHTS):
            row = OUT_BIAS_ROW + HALVES * w
            nc.scalar.dma_start(
                out=vec_rows[row : row + HALVES, :],
                in_=out_bias_vectors[w].rearrange("(r c) -> r c", c=N_TILE),
            )

        identity = keep.tile([P, P], F32)
        masks.make_identity(nc, identity[:])
        identity_bf = keep.tile([P, P], BF16)
        masks.make_identity(nc, identity_bf[:])

        chunk_words = {}

        def load_columns(c, lo, hi):
            source = weight_words[c // GROUPS][c % GROUPS].rearrange("p n t -> p (n t)")
            cols = slice(PACK * lo, PACK * hi)
            nc.sync.dma_start(
                out=chunk_words[c][:, cols].bitcast(I32), in_=source[:, cols].bitcast(I32)
            )

        def load_chunk(c):
            chunk_words[c] = ring.tile([P, PACK * A], U8, name="words", align_bytes=4096)
            if c < CHUNKS - LATE:
                load_columns(c, 0, A)
                return
            load_columns(c, 0, N_TILE)
            if c == CHUNKS - 1:
                for late in range(CHUNKS - LATE, CHUNKS):
                    pieces = COLUMNS[-1][1:] if late == CHUNKS - 1 else [A - N_TILE]
                    start = N_TILE
                    for width in pieces:
                        load_columns(late, start, start + width)
                        start += width

        for c in range(RING):
            load_chunk(c)

        vec_sorted = keep.tile([P, PACK, P], F32)
        nc.scalar.copy(out=vec_sorted[:], in_=vec_rows[:].rearrange("r (p t) -> r t p", t=PACK))
        vec_flipped = flip_banks.tile([P, PACK, P], F32, tag="flip")
        for t in range(PACK):
            nc.tensor.transpose(vec_flipped[:, t, :], vec_sorted[:, t, :], identity[:])
        gain_bias = keep.tile([P, PACK, 2 * GROUPS], F32)
        nc.scalar.copy(out=gain_bias[:], in_=vec_flipped[:, :, 0 : 2 * GROUPS])

        out_bias = keep.tile([P, WEIGHTS * A], F32)
        for j in range(WEIGHTS * HALVES):
            r = OUT_BIAS_ROW + j
            spread = flip_banks.tile([P, N_TILE], F32, tag="flip")
            nc.tensor.matmul(
                out=spread[:],
                lhsT=identity_bf[:, r : r + 1].to_broadcast([P, P]),
                rhs=vec_rows[:],
                start=True,
                stop=True,
            )
            nc.scalar.copy(out=out_bias[:, j * N_TILE : (j + 1) * N_TILE], in_=spread[:])

        stats = keep.tile([P, X_TILES * STATS_PER_TILE, 6], F32)

        def take_statistics(i):
            for j in range(STATS_PER_TILE):
                nc.vector.bn_stats(
                    out=stats[:, i * STATS_PER_TILE + j, :],
                    in_=x_tiles[i][:, j * STAT_COLS : (j + 1) * STAT_COLS],
                )

        take_statistics(0)

        planes = keep.tile([P, WEIGHTS, BLOCKS, A], U8, align_bytes=1024)
        nc.vector.memset(planes[:].rearrange("p w j n -> p (w j n)").bitcast(I32), 0)

        for w in range(WEIGHTS):
            for j in range(BLOCKS):
                last = j == BLOCKS - 1
                groups = BLOCK if last else 2 * BLOCK
                for quadrant in (0, 1, 2, 3) if last else (0, 2, 1, 3):
                    nc.gpsimd.dma_start(
                        out=planes[
                            32 * quadrant : 32 * quadrant + 4 * groups, w, j, :
                        ].bitcast(F32),
                        in_=weight_scales[w][
                            BLOCK * j : BLOCK * j + groups, 4 * quadrant : 4 * quadrant + 4, :
                        ].bitcast(F32),
                    )

        take_statistics(1)
        mean_var = keep.tile([P, 2], F32)
        nc.vector.bn_aggr(out=mean_var[:], in_=stats[:].rearrange("p c s -> p (c s)"))
        var_eps = keep.tile([P, 1], F32)
        nc.vector.tensor_scalar_add(out=var_eps[:], in0=mean_var[:, 1:2], scalar1=EPS)
        std = keep.tile([P, 1], F32)
        nc.scalar.sqrt(std[:], var_eps[:])
        rstd = keep.tile([P, 1], F32)
        nc.vector.reciprocal(out=rstd[:], in_=std[:])
        shift = keep.tile([P, 1], F32)
        nc.vector.scalar_tensor_tensor(
            out=shift[:], in0=mean_var[:, 0:1], scalar=-1.0, in1=rstd[:], op0=ALU.mult, op1=ALU.mult
        )

        h_words = keep.tile([P, GROUPS, P], U32, align_bytes=64)
        h_scales = keep.tile([P, GROUPS, P], U8, align_bytes=64)
        scaled_tiles = {}
        grouped_tiles = {}

        def normalise_flip_scale(b):
            scaled = stage.tile([P, BLOCK, PACK, P], BF16)
            for i in range(BLOCK):
                g = b * BLOCK + i
                normal = normals.tile([P, PACK, P], F32)
                nc.scalar.activation(
                    out=normal[:],
                    in_=x_tiles[g // X_GROUPS][
                        :, g % X_GROUPS * K_PASS : (g % X_GROUPS + 1) * K_PASS
                    ].rearrange("m (p t) -> m t p", t=PACK),
                    func=ACT.Identity,
                    bias=shift[:],
                    scale=rstd[:],
                )
                flipped = flip_banks.tile([P, PACK, P], F32, tag="flip")
                for t in range(PACK):
                    nc.tensor.transpose(flipped[:, t, :], normal[:, t, :], identity[:])
                for t in range(PACK):
                    nc.vector.tensor_scalar(
                        out=scaled[:, i, t, :],
                        in0=flipped[:, t, :],
                        scalar1=gain_bias[:, t, GAIN_ROW + g : GAIN_ROW + g + 1],
                        scalar2=gain_bias[:, t, BIAS_ROW + g : BIAS_ROW + g + 1],
                        op0=ALU.mult,
                        op1=ALU.add,
                    )
            scaled_tiles[b] = scaled

        def regroup(b):
            grouped = stage.tile([P, BLOCK, P, PACK], BF16, align_bytes=64)
            nc.vector.tensor_copy(
                out=grouped[:], in_=scaled_tiles[b][:].rearrange("p i t m -> p i m t")
            )
            grouped_tiles[b] = grouped

        def quantise(b):
            groups = slice(b * BLOCK, (b + 1) * BLOCK)
            nc.vector.quantize_mx(
                out=h_words[:, groups, :].rearrange("p i m -> p (i m)").bitcast(FP8X4),
                scales=h_scales[:, groups, :].rearrange("p i m -> p (i m)"),
                in_=grouped_tiles[b][:].rearrange("p i m t -> p (i m t)"),
            )

        sums = {}

        def open_sums(w):
            sums[w] = []
            start = 0
            for i, width in enumerate(COLUMNS[w]):
                if i < HALVES:
                    bank = sum_banks.tile([P, N_TILE], F32, name="sum", tag="sum")
                else:
                    bank = flip_banks.tile([P, N_TILE], F32, name="flip", tag="flip")
                sums[w].append((start, start + width, bank[:, 0:width]))
                start += width

        def project(w, g, pieces=slice(None)):
            c = w * GROUPS + g
            words = chunk_words[c]
            for lo, hi, sum_of_piece in sums[w][pieces]:
                nc.tensor.matmul_mx(
                    out=sum_of_piece,
                    lhsT=h_words[:, g, :].bitcast(FP8X4),
                    lhsT_scale=h_scales[:, g, :],
                    rhs=words[:, PACK * lo : PACK * hi].bitcast(FP8X4),
                    rhs_scale=planes[4 * (g % BLOCK) : P, w, g // BLOCK, lo:hi],
                    start=(g == 0),
                    stop=(g == GROUPS - 1),
                )
            if c + RING < CHUNKS:
                load_chunk(c + RING)

        def add_bias_and_store(w):
            result = results.tile([P, A], F32, align_bytes=1024)
            for lo, hi, sum_of_piece in sums[w]:
                nc.vector.tensor_tensor(
                    out=result[:, lo:hi],
                    in0=sum_of_piece,
                    in1=out_bias[:, w * A + lo : w * A + hi],
                    op=ALU.add,
                )
                if w == WEIGHTS - 1:
                    nc.scalar.dma_start(out=out_rows[w][:, lo:hi], in_=result[:, lo:hi])
            if w < WEIGHTS - 1:
                nc.sync.dma_start(out=out_rows[w], in_=result[:])

        open_sums(0)
        for b in range(BLOCKS + 2):
            if b < BLOCKS:
                normalise_flip_scale(b)
            if 1 <= b <= BLOCKS:
                quantise(b - 1)
            if b < BLOCKS:
                regroup(b)
            if b >= 2:
                for i in range(BLOCK):
                    project(0, (b - 2) * BLOCK + i)
        add_bias_and_store(0)

        for w in range(1, WEIGHTS):
            open_sums(w)
            late = LATE if w == WEIGHTS - 1 else 0
            for g in range(GROUPS - late):
                project(w, g)
            for pieces in [slice(0, 1), slice(1, None)]:
                for g in range(GROUPS - late, GROUPS):
                    project(w, g, pieces)
            add_bias_and_store(w)
